import numpy as np
import ml_dtypes


def mxq(x, axis, fmt="e4m3"):
    dtype, down = {"e4m3": (ml_dtypes.float8_e4m3fn, 7), "e5m2": (ml_dtypes.float8_e5m2, 14)}[fmt]
    v = np.moveaxis(np.asarray(x, np.float32).astype(ml_dtypes.bfloat16).astype(np.float64), axis, -1)
    blocks = v.reshape(v.shape[:-1] + (-1, 32))
    amax = np.abs(blocks).max(-1, keepdims=True)
    byte = np.maximum(np.where(amax > 0, np.frexp(amax)[1] - 1 + 127, 0) - down, 1)
    scale = np.exp2(byte - 127.0)
    codes = (blocks / scale).astype(np.float32).astype(dtype).astype(np.float64)
    return np.moveaxis((codes * scale).reshape(v.shape), -1, axis)


WIDE = False


def mx_kscale(k):
    if not WIDE:
        return np.ones(k)
    levels = np.array([10, -10, 5, -5, 0])
    if k % 512:
        return np.exp2(np.random.permutation(np.resize(levels, k // 32))).repeat(32)
    a = np.empty((k // 512, 16))
    for p in range(k // 512):
        a[p, :8] = np.random.permutation(np.resize(levels, 8))
        for g in range(8):
            far = levels[np.abs(levels - a[p, g]) >= 10]
            a[p, g + 8] = far[np.random.randint(len(far))]
    return np.exp2(a.ravel()).repeat(32)


BF16 = ml_dtypes.bfloat16


def bf(x):
    return np.asarray(x, np.float32).astype(BF16)


def f64(x):
    return np.asarray(x).astype(np.float64)


B, N, E, H, G, C, EO = 16, 512, 256, 2, 128, 512, 1024
D = E // H
NB = N // C


def silu(v):
    return v / (1.0 + np.exp(-v))


def setup_inputs():
    s = mx_kscale(N)
    return {"q": bf(silu(0.4 * np.random.standard_normal((B, H, N, D)))),
            "k": bf(silu(0.4 * np.random.standard_normal((B, H, N, D))) * s[:, None]),
            "v": bf(silu(0.4 * np.random.standard_normal((B, H, N, D))) / s[:, None]),
            "log_slope": bf(-(3.0 + 5.0 * np.random.random(H)) / N)}


def reference(q, k, v, log_slope):
    ls = f64(log_slope)
    vq = mxq(f64(v), 2, "e4m3")
    idx = np.arange(N, dtype=np.float64)
    outs = []
    for i in range(NB):
        lo, hi = i * C, (i + 1) * C
        diff = idx[lo:hi, None] - idx[None, :hi]
        decay = np.where(diff >= 0, np.exp(ls[:, None, None] * np.maximum(diff, 0.0)), 0.0)
        energy = (f64(q)[:, :, lo:hi] @ f64(k)[:, :, :hi].transpose(0, 1, 3, 2)) * decay
        outs.append(mxq(energy, 3, "e4m3") @ vq[:, :, :hi])
    return np.concatenate(outs, axis=2)

@@ -1,0 +1,172 @@
+from contextlib import ExitStack
+
+import concourse.mybir as mybir
+from concourse.masks import make_identity
+
+BF16 = mybir.dt.bfloat16
+F32 = mybir.dt.float32
+I32 = mybir.dt.int32
+U32 = mybir.dt.uint32
+U8 = mybir.dt.uint8
+FP8X4 = mybir.dt.float8_e4m3fn_x4
+
+P = 128
+PACK = 4
+BATCHES = 16
+HEADS = 2
+SEQ = 512
+WIDTH = 128
+KEY_TILES = SEQ // P
+CLASSES = SEQ // P
+BANDS = SEQ // P
+BAND_ROWS = P // BANDS
+ALL_HEADS = BATCHES * HEADS
+
+FLOPS = 2 * 2 * ALL_HEADS * SEQ * SEQ * WIDTH
+
+
+def tile_tnlattention_pa_t_kernel(tc, q, k, v, log_slope, out):
+    nc = tc.nc
+    with ExitStack() as ctx:
+        const = ctx.enter_context(tc.tile_pool(name="const", bufs=1))
+        resident = ctx.enter_context(tc.tile_pool(name="resident", bufs=1))
+        work = ctx.enter_context(tc.tile_pool(name="work", bufs=3))
+        psum_t = ctx.enter_context(tc.psum_pool(name="psum_t", bufs=2))
+        psum_e = ctx.enter_context(tc.psum_pool(name="psum_e", bufs=4))
+        psum_o = ctx.enter_context(tc.psum_pool(name="psum_o", bufs=2))
+        ctx.enter_context(tc.manual_schedule())
+
+        slope_bf = const.tile([P, HEADS], BF16)
+        nc.scalar.dma_start(out=slope_bf[:], in_=log_slope.partition_broadcast(P))
+        q_sb, k_sb, v_sb = [], [], []
+        for b in range(BATCHES):
+            q_sb.append(resident.tile([P, HEADS, CLASSES, WIDTH], BF16, name="q%d" % b))
+            k_sb.append(resident.tile([P, HEADS, KEY_TILES, WIDTH], BF16, name="k%d" % b))
+            v_sb.append(resident.tile([P, HEADS, KEY_TILES, WIDTH], BF16, name="v%d" % b))
+            nc.sync.dma_start(out=q_sb[b][:], in_=q[b].rearrange("h (m c) d -> m h c d", c=CLASSES))
+            nc.sync.dma_start(out=k_sb[b][:], in_=k[b].rearrange("h (p t) d -> p h t d", t=PACK))
+            nc.sync.dma_start(out=v_sb[b][:], in_=v[b].rearrange("h (p t) d -> p h t d", t=PACK))
+
+        distance_int = const.tile([P, BANDS * SEQ], I32)
+        nc.gpsimd.iota(
+            distance_int[:],
+            pattern=[[P, BANDS], [1, CLASSES], [PACK, BAND_ROWS], [-1, PACK]],
+            base=0,
+            channel_multiplier=-PACK,
+        )
+        identity = const.tile([P, P], BF16)
+        make_identity(nc, identity[:])
+
+        slope = const.tile([P, HEADS], F32)
+        nc.vector.tensor_copy(out=slope[:], in_=slope_bf[:])
+        distance = const.tile([P, BANDS * SEQ], F32)
+        nc.vector.tensor_copy(out=distance[:], in_=distance_int[:])
+        not_later = const.tile([P, BANDS * SEQ], F32)
+        nc.vector.tensor_single_scalar(out=not_later[:], in_=distance[:], scalar=0.0, op=mybir.AluOpType.is_ge)
+        nc.vector.tensor_scalar_max(out=distance[:], in0=distance[:], scalar1=0.0)
+
+        decay = const.tile([P, HEADS, BANDS, CLASSES, BAND_ROWS, PACK], F32)
+        grouped = []
+        for h in range(HEADS):
+            decay_h = decay[:, h, :, :, :, :].rearrange("p s c r t -> p (s c r t)")
+            nc.scalar.activation(
+                out=decay_h,
+                in_=distance[:],
+                func=mybir.ActivationFunctionType.Exp,
+                scale=slope[:, h : h + 1],
+            )
+            grouped.append(const.tile([P, CLASSES, P, PACK], BF16, name="grouped%d" % h, align_bytes=64))
+            nc.vector.tensor_tensor(out=decay_h, in0=decay_h, in1=not_later[:], op=mybir.AluOpType.mult)
+
+        qk_t = {}
+        e_words, e_scales = {}, {}
+        v_grouped, v_words, v_scales = {}, {}, {}
+
+        def transpose_q_k(head):
+            b, h = divmod(head, HEADS)
+            flipped = psum_t.tile([P, 2, PACK, P], BF16)
+            for c in range(CLASSES):
+                nc.tensor.transpose(flipped[:, 0, c, :], q_sb[b][:, h, c, :], identity[:])
+            for t in range(KEY_TILES):
+                nc.tensor.transpose(flipped[:, 1, t, :], k_sb[b][:, h, t, :], identity[:])
+            qk_t[head] = work.tile([P, 2, PACK, P], BF16, name="qk_t")
+            nc.scalar.copy(out=qk_t[head][:], in_=flipped[:])
+
+        def regroup_v(b):
+            v_grouped[b] = work.tile([P, HEADS, WIDTH, PACK], BF16, name="v_grouped", align_bytes=64)
+            nc.scalar.copy(out=v_grouped[b][:], in_=v_sb[b][:].rearrange("p h t d -> p h d t"))
+
+        def quantise_v(b):
+            v_words[b] = work.tile([P, HEADS * WIDTH], U32, name="v_words", align_bytes=64)
+            v_scales[b] = work.tile([P, HEADS * WIDTH], U8, name="v_scales", align_bytes=64)
+            nc.vector.quantize_mx(
+                out=v_words[b][:].bitcast(FP8X4),
+                scales=v_scales[b][:],
+                in_=v_grouped[b][:].rearrange("p h d t -> p (h d t)"),
+            )
+
+        def energy_of_band(head, s):
+            h = head % HEADS
+            rows = slice(s * BAND_ROWS, (s + 1) * BAND_ROWS)
+            product = psum_e.tile([P, KEY_TILES, CLASSES, BAND_ROWS], F32)
+            for t in range(KEY_TILES):
+                nc.tensor.matmul(
+                    out=product[:, t, :, :],
+                    lhsT=qk_t[head][:, 1, t, :],
+                    rhs=qk_t[head][:, 0, :, rows],
+                    start=True,
+                    stop=True,
+                )
+            nc.vector.tensor_tensor(
+                out=grouped[h][:, :, rows, :],
+                in0=product[:].rearrange("p t c r -> p c r t"),
+                in1=decay[:, h, s, :, :, :],
+                op=mybir.AluOpType.mult,
+            )
+
+        def quantise_energy(head):
+            e_words[head] = work.tile([P, SEQ], U32, name="e_words", align_bytes=64)
+            e_scales[head] = work.tile([P, SEQ], U8, name="e_scales", align_bytes=64)
+            nc.vector.quantize_mx(
+                out=e_words[head][:].bitcast(FP8X4),
+                scales=e_scales[head][:],
+                in_=grouped[head % HEADS][:].rearrange("p c m t -> p (c m t)"),
+            )
+
+        def output(head):
+            b, h = divmod(head, HEADS)
+            columns = slice(h * WIDTH, (h + 1) * WIDTH)
+            result = psum_o.tile([P, CLASSES, WIDTH], F32)
+            for c in range(CLASSES):
+                queries = slice(c * P, (c + 1) * P)
+                nc.tensor.matmul_mx(
+                    out=result[:, c, :],
+                    lhsT=e_words[head][:, queries].bitcast(FP8X4),
+                    lhsT_scale=e_scales[head][:, queries],
+                    rhs=v_words[b][:, columns].bitcast(FP8X4),
+                    rhs_scale=v_scales[b][:, columns],
+                    start=True,
+                    stop=True,
+                )
+            out_sb = resident.tile([P, CLASSES, WIDTH], F32, name="out%d" % head)
+            nc.scalar.copy(out=out_sb[:], in_=result[:])
+            nc.sync.dma_start(out=out[b, h].rearrange("(m c) d -> m c d", c=CLASSES), in_=out_sb[:])
+
+        for step in range(ALL_HEADS + 3):
+            if step >= 3:
+                output(step - 3)
+            if step < ALL_HEADS:
+                transpose_q_k(step)
+                if step % HEADS == 0:
+                    regroup_v(step // HEADS)
+            has_energy = 1 <= step <= ALL_HEADS
+            if has_energy:
+                energy_of_band(step - 1, 0)
+            if 2 <= step <= ALL_HEADS + 1:
+                quantise_energy(step - 2)
+            if has_energy:
+                energy_of_band(step - 1, 1)
+                if step % HEADS == 1:
+                    quantise_v(step // HEADS)
+                energy_of_band(step - 1, 2)
+                energy_of_band(step - 1, 3)

@@ -11,18 +11,21 @@ U8 = mybir.dt.uint8
 FP8X4 = mybir.dt.float8_e4m3fn_x4
 
 P = 128
+HALF_P = P // 2
 PACK = 4
 BATCHES = 16
 HEADS = 2
 SEQ = 512
 WIDTH = 128
-KEY_TILES = SEQ // P
-CLASSES = SEQ // P
-BANDS = SEQ // P
-BAND_ROWS = P // BANDS
-ALL_HEADS = BATCHES * HEADS
+HALVES = 2
+CLASSES = 2
+HALF_SEQ = SEQ // HALVES
+KINDS = 1 + HEADS
+TILES = KINDS * CLASSES
+PAIR = 2
+BUFS = 3
 
-FLOPS = 2 * 2 * ALL_HEADS * SEQ * SEQ * WIDTH
+FLOPS = 2 * 2 * BATCHES * HEADS * SEQ * SEQ * WIDTH
 
 
 def tile_tnlattention_pa_t_kernel(tc, q, k, v, log_slope, out):
@@ -30,7 +33,7 @@ def tile_tnlattention_pa_t_kernel(tc, q, k, v, log_slope, out):
     with ExitStack() as ctx:
         const = ctx.enter_context(tc.tile_pool(name="const", bufs=1))
         resident = ctx.enter_context(tc.tile_pool(name="resident", bufs=1))
-        work = ctx.enter_context(tc.tile_pool(name="work", bufs=3))
+        work = ctx.enter_context(tc.tile_pool(name="work", bufs=BUFS))
         psum_t = ctx.enter_context(tc.psum_pool(name="psum_t", bufs=2))
         psum_e = ctx.enter_context(tc.psum_pool(name="psum_e", bufs=4))
         psum_o = ctx.enter_context(tc.psum_pool(name="psum_o", bufs=2))
@@ -40,133 +43,209 @@ def tile_tnlattention_pa_t_kernel(tc, q, k, v, log_slope, out):
         nc.scalar.dma_start(out=slope_bf[:], in_=log_slope.partition_broadcast(P))
         q_sb, k_sb, v_sb = [], [], []
         for b in range(BATCHES):
-            q_sb.append(resident.tile([P, HEADS, CLASSES, WIDTH], BF16, name="q%d" % b))
-            k_sb.append(resident.tile([P, HEADS, KEY_TILES, WIDTH], BF16, name="k%d" % b))
-            v_sb.append(resident.tile([P, HEADS, KEY_TILES, WIDTH], BF16, name="v%d" % b))
-            nc.sync.dma_start(out=q_sb[b][:], in_=q[b].rearrange("h (m c) d -> m h c d", c=CLASSES))
-            nc.sync.dma_start(out=k_sb[b][:], in_=k[b].rearrange("h (p t) d -> p h t d", t=PACK))
-            nc.sync.dma_start(out=v_sb[b][:], in_=v[b].rearrange("h (p t) d -> p h t d", t=PACK))
-
-        distance_int = const.tile([P, BANDS * SEQ], I32)
-        nc.gpsimd.iota(
-            distance_int[:],
-            pattern=[[P, BANDS], [1, CLASSES], [PACK, BAND_ROWS], [-1, PACK]],
-            base=0,
-            channel_multiplier=-PACK,
-        )
-        identity = const.tile([P, P], BF16)
-        make_identity(nc, identity[:])
-
-        slope = const.tile([P, HEADS], F32)
-        nc.vector.tensor_copy(out=slope[:], in_=slope_bf[:])
-        distance = const.tile([P, BANDS * SEQ], F32)
-        nc.vector.tensor_copy(out=distance[:], in_=distance_int[:])
-        not_later = const.tile([P, BANDS * SEQ], F32)
-        nc.vector.tensor_single_scalar(out=not_later[:], in_=distance[:], scalar=0.0, op=mybir.AluOpType.is_ge)
-        nc.vector.tensor_scalar_max(out=distance[:], in0=distance[:], scalar1=0.0)
-
-        decay = const.tile([P, HEADS, BANDS, CLASSES, BAND_ROWS, PACK], F32)
-        grouped = []
-        for h in range(HEADS):
-            decay_h = decay[:, h, :, :, :, :].rearrange("p s c r t -> p (s c r t)")
-            nc.scalar.activation(
-                out=decay_h,
-                in_=distance[:],
-                func=mybir.ActivationFunctionType.Exp,
-                scale=slope[:, h : h + 1],
+            q_sb.append(resident.tile([P, HEADS * HALVES, CLASSES, WIDTH], BF16, name="q%d" % b))
+            k_sb.append(resident.tile([P, HEADS, PACK, WIDTH], BF16, name="k%d" % b))
+            nc.sync.dma_start(
+                out=q_sb[b][:],
+                in_=q[b].rearrange("h n d -> (h n) d").rearrange("(g m c) d -> m g c d", m=P, c=CLASSES),
             )
-            grouped.append(const.tile([P, CLASSES, P, PACK], BF16, name="grouped%d" % h, align_bytes=64))
-            nc.vector.tensor_tensor(out=decay_h, in0=decay_h, in1=not_later[:], op=mybir.AluOpType.mult)
+            nc.sync.dma_start(out=k_sb[b][:], in_=k[b].rearrange("h (p t) d -> p h t d", t=PACK))
+            if b % PAIR == 0:
+                v_sb.append(resident.tile([P, HEADS, PAIR, PACK, WIDTH], BF16, name="v%d" % b))
+                pair = v[b : b + PAIR]
+                target = v_sb[b // PAIR]
+                nc.sync.dma_start(out=target[:, 0, :, :, :], in_=pair[:, 0].rearrange("b (p t) d -> p b t d", t=PACK))
+                for x in range(2):
+                    nc.sync.dma_start(
+                        out=target[x * HALF_P : (x + 1) * HALF_P, 1, :, :, :],
+                        in_=pair[:, 1, (1 - x) * HALF_SEQ : (2 - x) * HALF_SEQ].rearrange(
+                            "b (p t) d -> p b t d", t=PACK
+                        ),
+                    )
+
+        identities = const.tile([P, 2, P], BF16)
+        make_identity(nc, identities[:, 0, :])
+        make_identity(nc, identities[:, 1, :])
+        identity = identities[:, 0, :]
+        exchange = identities[:].rearrange("p a n -> p (a n)")[:, HALF_P : HALF_P + P]
+        ramp = const.tile([P, CLASSES * P * PACK], I32)
+        nc.gpsimd.iota(
+            ramp[:], pattern=[[1, CLASSES], [CLASSES, P], [-1, PACK]], base=0, channel_multiplier=-PACK
+        )
+        nearer = const.tile([P, KINDS], F32)
+        nc.vector.memset(nearer[:], 0.0)
+        nc.vector.memset(nearer[HALF_P:P, 0:1], -float(HALF_SEQ))
+        nc.vector.memset(nearer[:, 1:2], -float(HALF_SEQ))
+        nc.vector.memset(nearer[HALF_P:P, 2:3], -float(SEQ))
+        k_half, v_half = [], []
+        for i in range(BUFS):
+            k_half.append(const.tile([P, HEADS, PACK, P], BF16, name="k_half%d" % i))
+            nc.vector.memset(k_half[i][:], 0.0)
+        for i in range(BUFS):
+            v_half.append(const.tile([P, HEADS, WIDTH], U32, name="v_half%d" % i, align_bytes=64))
+            nc.vector.memset(v_half[i][:], 0)
+        slope = const.tile([P, KINDS], F32)
+        nc.vector.tensor_copy(out=slope[:, 1:KINDS], in_=slope_bf[:])
+        nc.vector.tensor_copy(out=slope[0:HALF_P, 0:1], in_=slope_bf[0:HALF_P, 0:1])
+        nc.vector.tensor_copy(out=slope[HALF_P:P, 0:1], in_=slope_bf[HALF_P:P, 1:2])
+        decay = const.tile([P, KINDS, CLASSES, P, PACK], F32)
+        for kind in range(KINDS):
+            nc.vector.tensor_scalar(
+                out=decay[:, kind, :, :, :].rearrange("p c m t -> p (c m t)"),
+                in0=ramp[:],
+                scalar1=nearer[:, kind : kind + 1],
+                scalar2=0.0,
+                op0=mybir.AluOpType.subtract,
+                op1=mybir.AluOpType.max,
+            )
+        for kind in range(KINDS):
+            flat = decay[:, kind, :, :, :].rearrange("p c m t -> p (c m t)")
+            nc.scalar.activation(
+                out=flat,
+                in_=flat,
+                func=mybir.ActivationFunctionType.Exp,
+                scale=slope[:, kind : kind + 1],
+            )
+            nc.vector.scalar_tensor_tensor(
+                out=flat,
+                in0=ramp[:],
+                scalar=nearer[:, kind : kind + 1],
+                in1=flat,
+                op0=mybir.AluOpType.is_ge,
+                op1=mybir.AluOpType.mult,
+            )
 
         qk_t = {}
+        grouped = {}
         e_words, e_scales = {}, {}
         v_grouped, v_words, v_scales = {}, {}, {}
 
-        def transpose_q_k(head):
-            b, h = divmod(head, HEADS)
-            flipped = psum_t.tile([P, 2, PACK, P], BF16)
-            for c in range(CLASSES):
-                nc.tensor.transpose(flipped[:, 0, c, :], q_sb[b][:, h, c, :], identity[:])
-            for t in range(KEY_TILES):
-                nc.tensor.transpose(flipped[:, 1, t, :], k_sb[b][:, h, t, :], identity[:])
-            qk_t[head] = work.tile([P, 2, PACK, P], BF16, name="qk_t")
-            nc.scalar.copy(out=qk_t[head][:], in_=flipped[:])
+        def transpose_q_k(b):
+            for h in range(HEADS):
+                flipped = psum_t.tile([P, 2, PACK, P], BF16)
+                for half in range(HALVES):
+                    for c in range(CLASSES):
+                        nc.tensor.transpose(
+                            flipped[:, 0, half * CLASSES + c, :], q_sb[b][:, h * HALVES + half, c, :], identity
+                        )
+                for t in range(PACK):
+                    nc.tensor.transpose(flipped[:, 1, t, :], k_sb[b][:, h, t, :], identity if h == 0 else exchange)
+                qk_t[b, h] = work.tile([P, 2, PACK, P], BF16, name="qk_t%d" % h)
+                nc.scalar.copy(out=qk_t[b, h][:], in_=flipped[:])
+                first_keys = slice(h * HALF_P, (h + 1) * HALF_P)
+                nc.scalar.copy(out=k_half[b % BUFS][:, h, :, first_keys], in_=flipped[:, 1, :, first_keys])
 
         def regroup_v(b):
             v_grouped[b] = work.tile([P, HEADS, WIDTH, PACK], BF16, name="v_grouped", align_bytes=64)
-            nc.scalar.copy(out=v_grouped[b][:], in_=v_sb[b][:].rearrange("p h t d -> p h d t"))
+            nc.scalar.copy(
+                out=v_grouped[b][:], in_=v_sb[b // PAIR][:, :, b % PAIR, :, :].rearrange("p h t d -> p h d t")
+            )
 
         def quantise_v(b):
-            v_words[b] = work.tile([P, HEADS * WIDTH], U32, name="v_words", align_bytes=64)
-            v_scales[b] = work.tile([P, HEADS * WIDTH], U8, name="v_scales", align_bytes=64)
+            v_words[b] = work.tile([P, HEADS, WIDTH], U32, name="v_words", align_bytes=64)
+            v_scales[b] = work.tile([P, HEADS, WIDTH], U8, name="v_scales", align_bytes=64)
             nc.vector.quantize_mx(
-                out=v_words[b][:].bitcast(FP8X4),
-                scales=v_scales[b][:],
+                out=v_words[b][:].rearrange("p h d -> p (h d)").bitcast(FP8X4),
+                scales=v_scales[b][:].rearrange("p h d -> p (h d)"),
                 in_=v_grouped[b][:].rearrange("p h d t -> p (h d t)"),
             )
 
-        def energy_of_band(head, s):
-            h = head % HEADS
-            rows = slice(s * BAND_ROWS, (s + 1) * BAND_ROWS)
-            product = psum_e.tile([P, KEY_TILES, CLASSES, BAND_ROWS], F32)
-            for t in range(KEY_TILES):
-                nc.tensor.matmul(
-                    out=product[:, t, :, :],
-                    lhsT=qk_t[head][:, 1, t, :],
-                    rhs=qk_t[head][:, 0, :, rows],
-                    start=True,
-                    stop=True,
-                )
+        def pad_v(b):
+            for h in range(HEADS):
+                rows = slice(h * HALF_P, (h + 1) * HALF_P)
+                nc.vector.tensor_copy(out=v_half[b % BUFS][rows, h, :], in_=v_words[b][rows, h, :])
+
+        def energy(b, kind, c):
+            product = psum_e.tile([P, PACK, P], F32)
+            for t in range(PACK):
+                if kind == 0:
+                    for h in range(HEADS):
+                        nc.tensor.matmul(
+                            out=product[:, t, :],
+                            lhsT=k_half[b % BUFS][:, h, t, :],
+                            rhs=qk_t[b, h][:, 0, c, :],
+                            start=(h == 0),
+                            stop=(h == HEADS - 1),
+                        )
+                else:
+                    nc.tensor.matmul(
+                        out=product[:, t, :],
+                        lhsT=qk_t[b, kind - 1][:, 1, t, :],
+                        rhs=qk_t[b, kind - 1][:, 0, CLASSES + c, :],
+                        start=True,
+                        stop=True,
+                    )
             nc.vector.tensor_tensor(
-                out=grouped[h][:, :, rows, :],
-                in0=product[:].rearrange("p t c r -> p c r t"),
-                in1=decay[:, h, s, :, :, :],
+                out=grouped[b][:, kind * CLASSES + c, :, :],
+                in0=product[:].rearrange("p t m -> p m t"),
+                in1=decay[:, kind, c, :, :],
                 op=mybir.AluOpType.mult,
             )
 
-        def quantise_energy(head):
-            e_words[head] = work.tile([P, SEQ], U32, name="e_words", align_bytes=64)
-            e_scales[head] = work.tile([P, SEQ], U8, name="e_scales", align_bytes=64)
+        def quantise_energy(b, first, last):
             nc.vector.quantize_mx(
-                out=e_words[head][:].bitcast(FP8X4),
-                scales=e_scales[head][:],
-                in_=grouped[head % HEADS][:].rearrange("p c m t -> p (c m t)"),
+                out=e_words[b][:, first * P : last * P].bitcast(FP8X4),
+                scales=e_scales[b][:, first * P : last * P],
+                in_=grouped[b][:, first:last, :, :].rearrange("p n m t -> p (n m t)"),
             )
 
-        def output(head):
-            b, h = divmod(head, HEADS)
-            columns = slice(h * WIDTH, (h + 1) * WIDTH)
-            result = psum_o.tile([P, CLASSES, WIDTH], F32)
+        def output(b):
+            shared = psum_o.tile([P, CLASSES, HEADS, WIDTH], F32, name="result")
             for c in range(CLASSES):
-                queries = slice(c * P, (c + 1) * P)
                 nc.tensor.matmul_mx(
-                    out=result[:, c, :],
-                    lhsT=e_words[head][:, queries].bitcast(FP8X4),
-                    lhsT_scale=e_scales[head][:, queries],
-                    rhs=v_words[b][:, columns].bitcast(FP8X4),
-                    rhs_scale=v_scales[b][:, columns],
+                    out=shared[:, c, :, :].rearrange("m h d -> m (h d)"),
+                    lhsT=e_words[b][:, c * P : (c + 1) * P].bitcast(FP8X4),
+                    lhsT_scale=e_scales[b][:, c * P : (c + 1) * P],
+                    rhs=v_half[b % BUFS][:].rearrange("p h d -> p (h d)").bitcast(FP8X4),
+                    rhs_scale=v_scales[b][:].rearrange("p h d -> p (h d)"),
                     start=True,
                     stop=True,
                 )
-            out_sb = resident.tile([P, CLASSES, WIDTH], F32, name="out%d" % head)
-            nc.scalar.copy(out=out_sb[:], in_=result[:])
-            nc.sync.dma_start(out=out[b, h].rearrange("(m c) d -> m c d", c=CLASSES), in_=out_sb[:])
+            own = psum_o.tile([P, HEADS, CLASSES, WIDTH], F32, name="result")
+            for h in range(HEADS):
+                for c in range(CLASSES):
+                    tile = (1 + h) * CLASSES + c
+                    nc.tensor.matmul_mx(
+                        out=own[:, h, c, :],
+                        lhsT=e_words[b][:, tile * P : (tile + 1) * P].bitcast(FP8X4),
+                        lhsT_scale=e_scales[b][:, tile * P : (tile + 1) * P],
+                        rhs=v_words[b][:, h, :].bitcast(FP8X4),
+                        rhs_scale=v_scales[b][:, h, :],
+                        start=True,
+                        stop=True,
+                    )
+            out_sb = resident.tile([P, HEADS, HALVES, CLASSES, WIDTH], F32, name="out%d" % b)
+            nc.scalar.copy(out=out_sb[:, :, 0, :, :], in_=shared[:].rearrange("m c h d -> m h c d"))
+            nc.scalar.copy(out=out_sb[:, :, 1, :, :], in_=own[:])
+            nc.sync.dma_start(
+                out=out[b].rearrange("h n d -> (h n) d").rearrange("(g m c) d -> m g c d", m=P, c=CLASSES),
+                in_=out_sb[:].rearrange("m h a c d -> m (h a) c d"),
+            )
 
-        for step in range(ALL_HEADS + 3):
+        for step in range(BATCHES + 3):
             if step >= 3:
                 output(step - 3)
-            if step < ALL_HEADS:
+            if step < BATCHES:
                 transpose_q_k(step)
-                if step % HEADS == 0:
-                    regroup_v(step // HEADS)
-            has_energy = 1 <= step <= ALL_HEADS
+                regroup_v(step)
+            b = step - 1
+            has_energy = 0 <= b < BATCHES
+            has_quantise = 0 <= b - 1 < BATCHES
             if has_energy:
-                energy_of_band(step - 1, 0)
-            if 2 <= step <= ALL_HEADS + 1:
-                quantise_energy(step - 2)
+                grouped[b] = work.tile([P, TILES, P, PACK], BF16, name="grouped", align_bytes=64)
+                energy(b, 0, 0)
+            if has_quantise:
+                e_words[b - 1] = work.tile([P, TILES * P], U32, name="e_words", align_bytes=64)
+                e_scales[b - 1] = work.tile([P, TILES * P], U8, name="e_scales", align_bytes=64)
+                quantise_energy(b - 1, 0, 2)
             if has_energy:
-                energy_of_band(step - 1, 1)
-                if step % HEADS == 1:
-                    quantise_v(step // HEADS)
-                energy_of_band(step - 1, 2)
-                energy_of_band(step - 1, 3)
+                energy(b, 0, 1)
+            if has_quantise:
+                quantise_energy(b - 1, 2, 6)
+            if has_energy:
+                energy(b, 1, 0)
+                quantise_v(b)
+                energy(b, 1, 1)
+                energy(b, 2, 0)
+                pad_v(b)
+                energy(b, 2, 1)

@@ -120,20 +120,19 @@ def tile_tnlattention_pa_t_kernel(tc, q, k, v, log_slope, out):
         e_words, e_scales = {}, {}
         v_grouped, v_words, v_scales = {}, {}, {}
 
-        def transpose_q_k(b):
-            for h in range(HEADS):
-                flipped = psum_t.tile([P, 2, PACK, P], BF16)
-                for half in range(HALVES):
-                    for c in range(CLASSES):
-                        nc.tensor.transpose(
-                            flipped[:, 0, half * CLASSES + c, :], q_sb[b][:, h * HALVES + half, c, :], identity
-                        )
-                for t in range(PACK):
-                    nc.tensor.transpose(flipped[:, 1, t, :], k_sb[b][:, h, t, :], identity if h == 0 else exchange)
-                qk_t[b, h] = work.tile([P, 2, PACK, P], BF16, name="qk_t%d" % h)
-                nc.scalar.copy(out=qk_t[b, h][:], in_=flipped[:])
-                first_keys = slice(h * HALF_P, (h + 1) * HALF_P)
-                nc.scalar.copy(out=k_half[b % BUFS][:, h, :, first_keys], in_=flipped[:, 1, :, first_keys])
+        def transpose_q_k(b, h):
+            flipped = psum_t.tile([P, 2, PACK, P], BF16)
+            for half in range(HALVES):
+                for c in range(CLASSES):
+                    nc.tensor.transpose(
+                        flipped[:, 0, half * CLASSES + c, :], q_sb[b][:, h * HALVES + half, c, :], identity
+                    )
+            for t in range(PACK):
+                nc.tensor.transpose(flipped[:, 1, t, :], k_sb[b][:, h, t, :], identity if h == 0 else exchange)
+            qk_t[b, h] = work.tile([P, 2, PACK, P], BF16, name="qk_t%d" % h)
+            nc.scalar.copy(out=qk_t[b, h][:], in_=flipped[:])
+            first_keys = slice(h * HALF_P, (h + 1) * HALF_P)
+            nc.scalar.copy(out=k_half[b % BUFS][:, h, :, first_keys], in_=flipped[:, 1, :, first_keys])
 
         def regroup_v(b):
             v_grouped[b] = work.tile([P, HEADS, WIDTH, PACK], BF16, name="v_grouped", align_bytes=64)
@@ -223,11 +222,6 @@ def tile_tnlattention_pa_t_kernel(tc, q, k, v, log_slope, out):
             )
 
         for step in range(BATCHES + 3):
-            if step >= 3:
-                output(step - 3)
-            if step < BATCHES:
-                transpose_q_k(step)
-                regroup_v(step)
             b = step - 1
             has_energy = 0 <= b < BATCHES
             has_quantise = 0 <= b - 1 < BATCHES
@@ -242,10 +236,19 @@ def tile_tnlattention_pa_t_kernel(tc, q, k, v, log_slope, out):
                 energy(b, 0, 1)
             if has_quantise:
                 quantise_energy(b - 1, 2, 6)
+            if step < BATCHES:
+                transpose_q_k(step, 0)
             if has_energy:
                 energy(b, 1, 0)
                 quantise_v(b)
                 energy(b, 1, 1)
+            if step < BATCHES:
+                transpose_q_k(step, 1)
+                regroup_v(step)
+            if has_energy:
                 energy(b, 2, 0)
                 pad_v(b)
+            if step >= 3:
+                output(step - 3)
+            if has_energy:
                 energy(b, 2, 1)

@@ -34,6 +34,7 @@ def tile_tnlattention_pa_t_kernel(tc, q, k, v, log_slope, out):
         const = ctx.enter_context(tc.tile_pool(name="const", bufs=1))
         resident = ctx.enter_context(tc.tile_pool(name="resident", bufs=1))
         work = ctx.enter_context(tc.tile_pool(name="work", bufs=BUFS))
+        store = ctx.enter_context(tc.tile_pool(name="store", bufs=6))
         psum_t = ctx.enter_context(tc.psum_pool(name="psum_t", bufs=2))
         psum_e = ctx.enter_context(tc.psum_pool(name="psum_e", bufs=4))
         psum_o = ctx.enter_context(tc.psum_pool(name="psum_o", bufs=2))
@@ -45,11 +46,14 @@ def tile_tnlattention_pa_t_kernel(tc, q, k, v, log_slope, out):
         for b in range(BATCHES):
             q_sb.append(resident.tile([P, HEADS * HALVES, CLASSES, WIDTH], BF16, name="q%d" % b))
             k_sb.append(resident.tile([P, HEADS, PACK, WIDTH], BF16, name="k%d" % b))
-            nc.sync.dma_start(
-                out=q_sb[b][:],
-                in_=q[b].rearrange("h n d -> (h n) d").rearrange("(g m c) d -> m g c d", m=P, c=CLASSES),
-            )
-            nc.sync.dma_start(out=k_sb[b][:], in_=k[b].rearrange("h (p t) d -> p h t d", t=PACK))
+            for heads in [slice(0, 1), slice(1, 2)] if b == 0 else [slice(0, HEADS)]:
+                nc.sync.dma_start(
+                    out=q_sb[b][:, heads.start * HALVES : heads.stop * HALVES, :, :],
+                    in_=q[b, heads].rearrange("h n d -> (h n) d").rearrange("(g m c) d -> m g c d", m=P, c=CLASSES),
+                )
+                nc.sync.dma_start(
+                    out=k_sb[b][:, heads, :, :], in_=k[b, heads].rearrange("h (p t) d -> p h t d", t=PACK)
+                )
             if b % PAIR == 0:
                 v_sb.append(resident.tile([P, HEADS, PAIR, PACK, WIDTH], BF16, name="v%d" % b))
                 pair = v[b : b + PAIR]
@@ -68,49 +72,53 @@ def tile_tnlattention_pa_t_kernel(tc, q, k, v, log_slope, out):
         make_identity(nc, identities[:, 1, :])
         identity = identities[:, 0, :]
         exchange = identities[:].rearrange("p a n -> p (a n)")[:, HALF_P : HALF_P + P]
-        ramp = const.tile([P, CLASSES * P * PACK], I32)
-        nc.gpsimd.iota(
-            ramp[:], pattern=[[1, CLASSES], [CLASSES, P], [-1, PACK]], base=0, channel_multiplier=-PACK
-        )
-        nearer = const.tile([P, KINDS], F32)
-        nc.vector.memset(nearer[:], 0.0)
-        nc.vector.memset(nearer[HALF_P:P, 0:1], -float(HALF_SEQ))
-        nc.vector.memset(nearer[:, 1:2], -float(HALF_SEQ))
-        nc.vector.memset(nearer[HALF_P:P, 2:3], -float(SEQ))
+        ramp = const.tile([P, P * PACK], I32)
+        nc.gpsimd.iota(ramp[:], pattern=[[CLASSES, P], [-1, PACK]], base=0, channel_multiplier=-PACK)
+        nearer = const.tile([P, CLASSES, KINDS], F32)
+        nc.vector.memset(nearer[:, 0, :], 0.0)
+        nc.vector.memset(nearer[HALF_P:P, 0, 0:1], -float(HALF_SEQ))
+        nc.vector.memset(nearer[:, 0, 1:2], -float(HALF_SEQ))
+        nc.vector.memset(nearer[HALF_P:P, 0, 2:3], -float(SEQ))
+        nc.vector.tensor_scalar_add(out=nearer[:, 1, :], in0=nearer[:, 0, :], scalar1=-1.0)
         k_half, v_half = [], []
         for i in range(BUFS):
             k_half.append(const.tile([P, HEADS, PACK, P], BF16, name="k_half%d" % i))
-            nc.vector.memset(k_half[i][:], 0.0)
+            nc.gpsimd.memset(k_half[i][:].rearrange("p h t n -> p (h t n)").bitcast(U32), 0)
         for i in range(BUFS):
             v_half.append(const.tile([P, HEADS, WIDTH], U32, name="v_half%d" % i, align_bytes=64))
-            nc.vector.memset(v_half[i][:], 0)
+            nc.gpsimd.memset(v_half[i][:], 0)
+        decay = const.tile([P, KINDS, CLASSES, P * PACK], F32)
         slope = const.tile([P, KINDS], F32)
-        nc.vector.tensor_copy(out=slope[:, 1:KINDS], in_=slope_bf[:])
-        nc.vector.tensor_copy(out=slope[0:HALF_P, 0:1], in_=slope_bf[0:HALF_P, 0:1])
-        nc.vector.tensor_copy(out=slope[HALF_P:P, 0:1], in_=slope_bf[HALF_P:P, 1:2])
-        decay = const.tile([P, KINDS, CLASSES, P, PACK], F32)
         for kind in range(KINDS):
-            nc.vector.tensor_scalar(
-                out=decay[:, kind, :, :, :].rearrange("p c m t -> p (c m t)"),
-                in0=ramp[:],
-                scalar1=nearer[:, kind : kind + 1],
-                scalar2=0.0,
-                op0=mybir.AluOpType.subtract,
-                op1=mybir.AluOpType.max,
-            )
-        for kind in range(KINDS):
-            flat = decay[:, kind, :, :, :].rearrange("p c m t -> p (c m t)")
-            nc.scalar.activation(
-                out=flat,
-                in_=flat,
-                func=mybir.ActivationFunctionType.Exp,
-                scale=slope[:, kind : kind + 1],
-            )
+            for c in range(CLASSES):
+                nc.vector.tensor_scalar(
+                    out=decay[:, kind, c, :],
+                    in0=ramp[:],
+                    scalar1=nearer[:, c, kind : kind + 1],
+                    scalar2=0.0,
+                    op0=mybir.AluOpType.subtract,
+                    op1=mybir.AluOpType.max,
+                )
+            if kind == 0:
+                nc.vector.tensor_copy(out=slope[0:HALF_P, 0:1], in_=slope_bf[0:HALF_P, 0:1])
+                nc.vector.tensor_copy(out=slope[HALF_P:P, 0:1], in_=slope_bf[HALF_P:P, 1:2])
+                nc.vector.tensor_copy(out=slope[:, 1:KINDS], in_=slope_bf[:])
+
+        def exp_decay(kind):
+            for c in range(CLASSES):
+                nc.scalar.activation(
+                    out=decay[:, kind, c, :],
+                    in_=decay[:, kind, c, :],
+                    func=mybir.ActivationFunctionType.Exp,
+                    scale=slope[:, kind : kind + 1],
+                )
+
+        def mask_decay(kind, c):
             nc.vector.scalar_tensor_tensor(
-                out=flat,
+                out=decay[:, kind, c, :],
                 in0=ramp[:],
-                scalar=nearer[:, kind : kind + 1],
-                in1=flat,
+                scalar=nearer[:, c, kind : kind + 1],
+                in1=decay[:, kind, c, :],
                 op0=mybir.AluOpType.is_ge,
                 op1=mybir.AluOpType.mult,
             )
@@ -177,7 +185,7 @@ def tile_tnlattention_pa_t_kernel(tc, q, k, v, log_slope, out):
             nc.vector.tensor_tensor(
                 out=grouped[b][:, kind * CLASSES + c, :, :],
                 in0=product[:].rearrange("p t m -> p m t"),
-                in1=decay[:, kind, c, :, :],
+                in1=decay[:, kind, c, :].rearrange("p (m t) -> p m t", t=PACK),
                 op=mybir.AluOpType.mult,
             )
 
@@ -188,7 +196,7 @@ def tile_tnlattention_pa_t_kernel(tc, q, k, v, log_slope, out):
                 in_=grouped[b][:, first:last, :, :].rearrange("p n m t -> p (n m t)"),
             )
 
-        def output(b):
+        def output_shared(b, out_sb):
             shared = psum_o.tile([P, CLASSES, HEADS, WIDTH], F32, name="result")
             for c in range(CLASSES):
                 nc.tensor.matmul_mx(
@@ -200,8 +208,11 @@ def tile_tnlattention_pa_t_kernel(tc, q, k, v, log_slope, out):
                     start=True,
                     stop=True,
                 )
+            nc.scalar.copy(out=out_sb[:, :, 0, :, :], in_=shared[:].rearrange("m c h d -> m h c d"))
+
+        def output_own(b, out_sb, heads, copy):
             own = psum_o.tile([P, HEADS, CLASSES, WIDTH], F32, name="result")
-            for h in range(HEADS):
+            for h in heads:
                 for c in range(CLASSES):
                     tile = (1 + h) * CLASSES + c
                     nc.tensor.matmul_mx(
@@ -213,42 +224,58 @@ def tile_tnlattention_pa_t_kernel(tc, q, k, v, log_slope, out):
                         start=True,
                         stop=True,
                     )
-            out_sb = resident.tile([P, HEADS, HALVES, CLASSES, WIDTH], F32, name="out%d" % b)
-            nc.scalar.copy(out=out_sb[:, :, 0, :, :], in_=shared[:].rearrange("m c h d -> m h c d"))
-            nc.scalar.copy(out=out_sb[:, :, 1, :, :], in_=own[:])
-            nc.sync.dma_start(
-                out=out[b].rearrange("h n d -> (h n) d").rearrange("(g m c) d -> m g c d", m=P, c=CLASSES),
-                in_=out_sb[:].rearrange("m h a c d -> m (h a) c d"),
-            )
+            some = slice(heads[0], heads[-1] + 1)
+            copy(out=out_sb[:, some, 1, :, :], in_=own[:, some, :, :])
 
-        for step in range(BATCHES + 3):
-            b = step - 1
-            has_energy = 0 <= b < BATCHES
-            has_quantise = 0 <= b - 1 < BATCHES
-            if has_energy:
-                grouped[b] = work.tile([P, TILES, P, PACK], BF16, name="grouped", align_bytes=64)
-                energy(b, 0, 0)
-            if has_quantise:
-                e_words[b - 1] = work.tile([P, TILES * P], U32, name="e_words", align_bytes=64)
-                e_scales[b - 1] = work.tile([P, TILES * P], U8, name="e_scales", align_bytes=64)
-                quantise_energy(b - 1, 0, 2)
-            if has_energy:
-                energy(b, 0, 1)
-            if has_quantise:
-                quantise_energy(b - 1, 2, 6)
-            if step < BATCHES:
-                transpose_q_k(step, 0)
-            if has_energy:
-                energy(b, 1, 0)
-                quantise_v(b)
-                energy(b, 1, 1)
-            if step < BATCHES:
-                transpose_q_k(step, 1)
-                regroup_v(step)
-            if has_energy:
-                energy(b, 2, 0)
-                pad_v(b)
-            if step >= 3:
-                output(step - 3)
-            if has_energy:
-                energy(b, 2, 1)
+        def rows_of_out(b):
+            return out[b].rearrange("h n d -> (h n) d").rearrange("(g m c) d -> m g c d", m=P, c=CLASSES)
+
+        def output(b):
+            out_sb = store.tile([P, HEADS, HALVES, CLASSES, WIDTH], F32, name="out_sb")
+            output_shared(b, out_sb)
+            output_own(b, out_sb, [0, 1], nc.scalar.copy)
+            nc.sync.dma_start(out=rows_of_out(b), in_=out_sb[:].rearrange("m h a c d -> m (h a) c d"))
+
+        exp_decay(0)
+        transpose_q_k(0, 0)
+        transpose_q_k(0, 1)
+        exp_decay(1)
+        exp_decay(2)
+        regroup_v(0)
+        for b in range(BATCHES):
+            final = b == BATCHES - 1
+            grouped[b] = work.tile([P, TILES, P, PACK], BF16, name="grouped", align_bytes=64)
+            e_words[b] = work.tile([P, TILES * P], U32, name="e_words", align_bytes=64)
+            e_scales[b] = work.tile([P, TILES * P], U8, name="e_scales", align_bytes=64)
+            for kind in range(KINDS):
+                for c in range(CLASSES):
+                    if b == 0:
+                        mask_decay(kind, c)
+                    energy(b, kind, c)
+                    spot = kind * CLASSES + c
+                    if spot == 0 and b >= 1:
+                        quantise_energy(b - 1, 0, 2)
+                    if spot == 1 and b >= 1:
+                        quantise_energy(b - 1, 2, 6)
+                    if spot < HEADS and not final:
+                        transpose_q_k(b + 1, spot)
+                    if spot == 1 and not final:
+                        regroup_v(b + 1)
+                    if spot == 2:
+                        quantise_v(b)
+                    if spot == 3 and b >= 2:
+                        output(b - 2)
+                    if spot == 4:
+                        pad_v(b)
+                    if final and spot in (2, 4):
+                        quantise_energy(b, spot - 2, spot)
+        quantise_energy(BATCHES - 1, 4, 6)
+        output(BATCHES - 2)
+        out_sb = store.tile([P, HEADS, HALVES, CLASSES, WIDTH], F32, name="out_sb")
+        rows = rows_of_out(BATCHES - 1)
+        output_shared(BATCHES - 1, out_sb)
+        for h in range(HEADS):
+            nc.sync.dma_start(out=rows[:, h * HALVES, :, :], in_=out_sb[:, h, 0, :, :])
+        for h in range(HEADS):
+            output_own(BATCHES - 1, out_sb, [h], nc.scalar.copy if h == 0 else nc.vector.tensor_copy)
+            nc.sync.dma_start(out=rows[:, h * HALVES + 1, :, :], in_=out_sb[:, h, 1, :, :])

@@ -123,24 +123,29 @@ def tile_tnlattention_pa_t_kernel(tc, q, k, v, log_slope, out):
                 op1=mybir.AluOpType.mult,
             )
 
+        flipped = {}
         qk_t = {}
         grouped = {}
         e_words, e_scales = {}, {}
         v_grouped, v_words, v_scales = {}, {}, {}
 
-        def transpose_q_k(b, h):
-            flipped = psum_t.tile([P, 2, PACK, P], BF16)
+        def transpose_q(b, h):
+            flipped[b, h] = psum_t.tile([P, 2, PACK, P], BF16, name="flipped")
             for half in range(HALVES):
                 for c in range(CLASSES):
                     nc.tensor.transpose(
-                        flipped[:, 0, half * CLASSES + c, :], q_sb[b][:, h * HALVES + half, c, :], identity
+                        flipped[b, h][:, 0, half * CLASSES + c, :], q_sb[b][:, h * HALVES + half, c, :], identity
                     )
+
+        def transpose_k(b, h):
             for t in range(PACK):
-                nc.tensor.transpose(flipped[:, 1, t, :], k_sb[b][:, h, t, :], identity if h == 0 else exchange)
+                nc.tensor.transpose(
+                    flipped[b, h][:, 1, t, :], k_sb[b][:, h, t, :], identity if h == 0 else exchange
+                )
             qk_t[b, h] = work.tile([P, 2, PACK, P], BF16, name="qk_t%d" % h)
-            nc.scalar.copy(out=qk_t[b, h][:], in_=flipped[:])
+            nc.scalar.copy(out=qk_t[b, h][:], in_=flipped[b, h][:])
             first_keys = slice(h * HALF_P, (h + 1) * HALF_P)
-            nc.scalar.copy(out=k_half[b % BUFS][:, h, :, first_keys], in_=flipped[:, 1, :, first_keys])
+            nc.scalar.copy(out=k_half[b % BUFS][:, h, :, first_keys], in_=flipped[b, h][:, 1, :, first_keys])
 
         def regroup_v(b):
             v_grouped[b] = work.tile([P, HEADS, WIDTH, PACK], BF16, name="v_grouped", align_bytes=64)
@@ -160,7 +165,7 @@ def tile_tnlattention_pa_t_kernel(tc, q, k, v, log_slope, out):
         def pad_v(b):
             for h in range(HEADS):
                 rows = slice(h * HALF_P, (h + 1) * HALF_P)
-                nc.vector.tensor_copy(out=v_half[b % BUFS][rows, h, :], in_=v_words[b][rows, h, :])
+                nc.gpsimd.tensor_copy(out=v_half[b % BUFS][rows, h, :], in_=v_words[b][rows, h, :])
 
         def energy(b, kind, c):
             product = psum_e.tile([P, PACK, P], F32)
@@ -237,8 +242,9 @@ def tile_tnlattention_pa_t_kernel(tc, q, k, v, log_slope, out):
             nc.sync.dma_start(out=rows_of_out(b), in_=out_sb[:].rearrange("m h a c d -> m (h a) c d"))
 
         exp_decay(0)
-        transpose_q_k(0, 0)
-        transpose_q_k(0, 1)
+        for h in range(HEADS):
+            transpose_q(0, h)
+            transpose_k(0, h)
         exp_decay(1)
         exp_decay(2)
         regroup_v(0)
@@ -257,16 +263,17 @@ def tile_tnlattention_pa_t_kernel(tc, q, k, v, log_slope, out):
                         quantise_energy(b - 1, 0, 2)
                     if spot == 1 and b >= 1:
                         quantise_energy(b - 1, 2, 6)
-                    if spot < HEADS and not final:
-                        transpose_q_k(b + 1, spot)
-                    if spot == 1 and not final:
-                        regroup_v(b + 1)
+                    if spot in (0, 2) and not final:
+                        transpose_q(b + 1, spot // 2)
+                    if spot in (1, 3) and not final:
+                        transpose_k(b + 1, spot // 2)
                     if spot == 2:
                         quantise_v(b)
-                    if spot == 3 and b >= 2:
-                        output(b - 2)
-                    if spot == 4:
                         pad_v(b)
+                        if not final:
+                            regroup_v(b + 1)
+                    if spot == 4 and b >= 2:
+                        output(b - 2)
                     if final and spot in (2, 4):
                         quantise_energy(b, spot - 2, spot)
         quantise_energy(BATCHES - 1, 4, 6)

@@ -22,6 +22,7 @@ CLASSES = 2
 HALF_SEQ = SEQ // HALVES
 KINDS = 1 + HEADS
 TILES = KINDS * CLASSES
+ORDER = [1, 0, 2]
 PAIR = 2
 BUFS = 3
 
@@ -35,9 +36,9 @@ def tile_tnlattention_pa_t_kernel(tc, q, k, v, log_slope, out):
         resident = ctx.enter_context(tc.tile_pool(name="resident", bufs=1))
         work = ctx.enter_context(tc.tile_pool(name="work", bufs=BUFS))
         store = ctx.enter_context(tc.tile_pool(name="store", bufs=6))
-        psum_t = ctx.enter_context(tc.psum_pool(name="psum_t", bufs=2))
-        psum_e = ctx.enter_context(tc.psum_pool(name="psum_e", bufs=4))
-        psum_o = ctx.enter_context(tc.psum_pool(name="psum_o", bufs=2))
+        psum_t = ctx.enter_context(tc.psum_pool(name="psum_t", bufs=1))
+        psum_e = ctx.enter_context(tc.psum_pool(name="psum_e", bufs=6))
+        psum_o = ctx.enter_context(tc.psum_pool(name="psum_o", bufs=1))
         ctx.enter_context(tc.manual_schedule())
 
         slope_bf = const.tile([P, HEADS], BF16)
@@ -89,7 +90,7 @@ def tile_tnlattention_pa_t_kernel(tc, q, k, v, log_slope, out):
             nc.gpsimd.memset(v_half[i][:], 0)
         decay = const.tile([P, KINDS, CLASSES, P * PACK], F32)
         slope = const.tile([P, KINDS], F32)
-        for kind in range(KINDS):
+        for kind in ORDER:
             for c in range(CLASSES):
                 nc.vector.tensor_scalar(
                     out=decay[:, kind, c, :],
@@ -99,7 +100,7 @@ def tile_tnlattention_pa_t_kernel(tc, q, k, v, log_slope, out):
                     op0=mybir.AluOpType.subtract,
                     op1=mybir.AluOpType.max,
                 )
-            if kind == 0:
+            if kind == ORDER[0]:
                 nc.vector.tensor_copy(out=slope[0:HALF_P, 0:1], in_=slope_bf[0:HALF_P, 0:1])
                 nc.vector.tensor_copy(out=slope[HALF_P:P, 0:1], in_=slope_bf[HALF_P:P, 1:2])
                 nc.vector.tensor_copy(out=slope[:, 1:KINDS], in_=slope_bf[:])
@@ -126,6 +127,7 @@ def tile_tnlattention_pa_t_kernel(tc, q, k, v, log_slope, out):
         flipped = {}
         qk_t = {}
         grouped = {}
+        out_sb = {}
         e_words, e_scales = {}, {}
         v_grouped, v_words, v_scales = {}, {}, {}
 
@@ -167,7 +169,8 @@ def tile_tnlattention_pa_t_kernel(tc, q, k, v, log_slope, out):
                 rows = slice(h * HALF_P, (h + 1) * HALF_P)
                 nc.gpsimd.tensor_copy(out=v_half[b % BUFS][rows, h, :], in_=v_words[b][rows, h, :])
 
-        def energy(b, kind, c):
+        def energy(b, spot):
+            kind, c = ORDER[spot // CLASSES], spot % CLASSES
             product = psum_e.tile([P, PACK, P], F32)
             for t in range(PACK):
                 if kind == 0:
@@ -188,7 +191,7 @@ def tile_tnlattention_pa_t_kernel(tc, q, k, v, log_slope, out):
                         stop=True,
                     )
             nc.vector.tensor_tensor(
-                out=grouped[b][:, kind * CLASSES + c, :, :],
+                out=grouped[b][:, spot, :, :],
                 in0=product[:].rearrange("p t m -> p m t"),
                 in1=decay[:, kind, c, :].rearrange("p (m t) -> p m t", t=PACK),
                 op=mybir.AluOpType.mult,
@@ -201,88 +204,97 @@ def tile_tnlattention_pa_t_kernel(tc, q, k, v, log_slope, out):
                 in_=grouped[b][:, first:last, :, :].rearrange("p n m t -> p (n m t)"),
             )
 
-        def output_shared(b, out_sb):
+        def tile_of(kind, c):
+            first = (ORDER.index(kind) * CLASSES + c) * P
+            return slice(first, first + P)
+
+        def output_shared(b):
             shared = psum_o.tile([P, CLASSES, HEADS, WIDTH], F32, name="result")
             for c in range(CLASSES):
+                columns = tile_of(0, c)
                 nc.tensor.matmul_mx(
                     out=shared[:, c, :, :].rearrange("m h d -> m (h d)"),
-                    lhsT=e_words[b][:, c * P : (c + 1) * P].bitcast(FP8X4),
-                    lhsT_scale=e_scales[b][:, c * P : (c + 1) * P],
+                    lhsT=e_words[b][:, columns].bitcast(FP8X4),
+                    lhsT_scale=e_scales[b][:, columns],
                     rhs=v_half[b % BUFS][:].rearrange("p h d -> p (h d)").bitcast(FP8X4),
                     rhs_scale=v_scales[b][:].rearrange("p h d -> p (h d)"),
                     start=True,
                     stop=True,
                 )
-            nc.scalar.copy(out=out_sb[:, :, 0, :, :], in_=shared[:].rearrange("m c h d -> m h c d"))
+            out_sb[b] = store.tile([P, HEADS, HALVES, CLASSES, WIDTH], F32, name="out_sb")
+            nc.scalar.copy(out=out_sb[b][:, :, 0, :, :], in_=shared[:].rearrange("m c h d -> m h c d"))
 
-        def output_own(b, out_sb, heads, copy):
+        def output_own(b, heads, copy):
             own = psum_o.tile([P, HEADS, CLASSES, WIDTH], F32, name="result")
             for h in heads:
                 for c in range(CLASSES):
-                    tile = (1 + h) * CLASSES + c
+                    columns = tile_of(1 + h, c)
                     nc.tensor.matmul_mx(
                         out=own[:, h, c, :],
-                        lhsT=e_words[b][:, tile * P : (tile + 1) * P].bitcast(FP8X4),
-                        lhsT_scale=e_scales[b][:, tile * P : (tile + 1) * P],
+                        lhsT=e_words[b][:, columns].bitcast(FP8X4),
+                        lhsT_scale=e_scales[b][:, columns],
                         rhs=v_words[b][:, h, :].bitcast(FP8X4),
                         rhs_scale=v_scales[b][:, h, :],
                         start=True,
                         stop=True,
                     )
             some = slice(heads[0], heads[-1] + 1)
-            copy(out=out_sb[:, some, 1, :, :], in_=own[:, some, :, :])
+            copy(out=out_sb[b][:, some, 1, :, :], in_=own[:, some, :, :])
 
         def rows_of_out(b):
             return out[b].rearrange("h n d -> (h n) d").rearrange("(g m c) d -> m g c d", m=P, c=CLASSES)
 
-        def output(b):
-            out_sb = store.tile([P, HEADS, HALVES, CLASSES, WIDTH], F32, name="out_sb")
-            output_shared(b, out_sb)
-            output_own(b, out_sb, [0, 1], nc.scalar.copy)
-            nc.sync.dma_start(out=rows_of_out(b), in_=out_sb[:].rearrange("m h a c d -> m (h a) c d"))
+        def store_out(b):
+            nc.sync.dma_start(out=rows_of_out(b), in_=out_sb[b][:].rearrange("m h a c d -> m (h a) c d"))
 
-        exp_decay(0)
-        for h in range(HEADS):
-            transpose_q(0, h)
-            transpose_k(0, h)
         exp_decay(1)
-        exp_decay(2)
-        regroup_v(0)
+        transpose_q(0, 0)
+        transpose_k(0, 0)
+        exp_decay(0)
+        last = BATCHES - 1
         for b in range(BATCHES):
-            final = b == BATCHES - 1
             grouped[b] = work.tile([P, TILES, P, PACK], BF16, name="grouped", align_bytes=64)
             e_words[b] = work.tile([P, TILES * P], U32, name="e_words", align_bytes=64)
             e_scales[b] = work.tile([P, TILES * P], U8, name="e_scales", align_bytes=64)
-            for kind in range(KINDS):
-                for c in range(CLASSES):
+            for spot in range(TILES):
+                if b == 0:
+                    mask_decay(ORDER[spot // CLASSES], spot % CLASSES)
+                energy(b, spot)
+                if spot == 0:
                     if b == 0:
-                        mask_decay(kind, c)
-                    energy(b, kind, c)
-                    spot = kind * CLASSES + c
-                    if spot == 0 and b >= 1:
-                        quantise_energy(b - 1, 0, 2)
-                    if spot == 1 and b >= 1:
-                        quantise_energy(b - 1, 2, 6)
-                    if spot in (0, 2) and not final:
-                        transpose_q(b + 1, spot // 2)
-                    if spot in (1, 3) and not final:
-                        transpose_k(b + 1, spot // 2)
-                    if spot == 2:
-                        quantise_v(b)
-                        pad_v(b)
-                        if not final:
-                            regroup_v(b + 1)
-                    if spot == 4 and b >= 2:
-                        output(b - 2)
-                    if final and spot in (2, 4):
-                        quantise_energy(b, spot - 2, spot)
-        quantise_energy(BATCHES - 1, 4, 6)
-        output(BATCHES - 2)
-        out_sb = store.tile([P, HEADS, HALVES, CLASSES, WIDTH], F32, name="out_sb")
-        rows = rows_of_out(BATCHES - 1)
-        output_shared(BATCHES - 1, out_sb)
+                        transpose_q(0, 1)
+                        transpose_k(0, 1)
+                        regroup_v(0)
+                        exp_decay(2)
+                    if b >= 1:
+                        quantise_energy(b - 1, 4, 6)
+                    if b >= 2:
+                        output_shared(b - 2)
+                if spot == 1 and b < last:
+                    transpose_q(b + 1, 0)
+                if spot == 2 and b < last:
+                    transpose_k(b + 1, 0)
+                if spot == 3:
+                    quantise_v(b)
+                    pad_v(b)
+                    if b >= 2:
+                        output_own(b - 2, [0, 1], nc.scalar.copy)
+                        store_out(b - 2)
+                if spot == 4:
+                    quantise_energy(b, 0, 4)
+                    if b < last:
+                        regroup_v(b + 1)
+                        transpose_q(b + 1, 1)
+                if spot == 5 and b < last:
+                    transpose_k(b + 1, 1)
+        quantise_energy(last, 4, 6)
+        output_shared(last - 1)
+        output_own(last - 1, [0, 1], nc.vector.tensor_copy)
+        store_out(last - 1)
+        rows = rows_of_out(last)
+        output_shared(last)
         for h in range(HEADS):
-            nc.sync.dma_start(out=rows[:, h * HALVES, :, :], in_=out_sb[:, h, 0, :, :])
+            nc.sync.dma_start(out=rows[:, h * HALVES, :, :], in_=out_sb[last][:, h, 0, :, :])
         for h in range(HEADS):
-            output_own(BATCHES - 1, out_sb, [h], nc.scalar.copy if h == 0 else nc.vector.tensor_copy)
-            nc.sync.dma_start(out=rows[:, h * HALVES + 1, :, :], in_=out_sb[:, h, 1, :, :])
+            output_own(last, [h], nc.vector.tensor_copy if h == 0 else nc.scalar.copy)
+            nc.sync.dma_start(out=rows[:, h * HALVES + 1, :, :], in_=out_sb[last][:, h, 1, :, :])

@@ -69,12 +69,12 @@ def tile_tnlattention_pa_t_kernel(tc, q, k, v, log_slope, out):
                     )
 
         identities = const.tile([P, 2, P], BF16)
+        ramp = const.tile([P, P * PACK], I32)
         make_identity(nc, identities[:, 0, :])
+        nc.gpsimd.iota(ramp[:], pattern=[[CLASSES, P], [-1, PACK]], base=0, channel_multiplier=-PACK)
         make_identity(nc, identities[:, 1, :])
         identity = identities[:, 0, :]
         exchange = identities[:].rearrange("p a n -> p (a n)")[:, HALF_P : HALF_P + P]
-        ramp = const.tile([P, P * PACK], I32)
-        nc.gpsimd.iota(ramp[:], pattern=[[CLASSES, P], [-1, PACK]], base=0, channel_multiplier=-PACK)
         nearer = const.tile([P, CLASSES, KINDS], F32)
         nc.vector.memset(nearer[:, 0, :], 0.0)
         nc.vector.memset(nearer[HALF_P:P, 0, 0:1], -float(HALF_SEQ))
@@ -84,10 +84,13 @@ def tile_tnlattention_pa_t_kernel(tc, q, k, v, log_slope, out):
         k_half, v_half = [], []
         for i in range(BUFS):
             k_half.append(const.tile([P, HEADS, PACK, P], BF16, name="k_half%d" % i))
-            nc.gpsimd.memset(k_half[i][:].rearrange("p h t n -> p (h t n)").bitcast(U32), 0)
-        for i in range(BUFS):
             v_half.append(const.tile([P, HEADS, WIDTH], U32, name="v_half%d" % i, align_bytes=64))
+
+        def zero(i):
+            nc.gpsimd.memset(k_half[i][:].rearrange("p h t n -> p (h t n)").bitcast(U32), 0)
             nc.gpsimd.memset(v_half[i][:], 0)
+
+        zero(0)
         decay = const.tile([P, KINDS, CLASSES, P * PACK], F32)
         slope = const.tile([P, KINDS], F32)
         for kind in ORDER:
@@ -101,9 +104,10 @@ def tile_tnlattention_pa_t_kernel(tc, q, k, v, log_slope, out):
                     op1=mybir.AluOpType.max,
                 )
             if kind == ORDER[0]:
+                nc.vector.tensor_copy(out=slope[:, 1:KINDS], in_=slope_bf[:])
+            if kind == ORDER[1]:
                 nc.vector.tensor_copy(out=slope[0:HALF_P, 0:1], in_=slope_bf[0:HALF_P, 0:1])
                 nc.vector.tensor_copy(out=slope[HALF_P:P, 0:1], in_=slope_bf[HALF_P:P, 1:2])
-                nc.vector.tensor_copy(out=slope[:, 1:KINDS], in_=slope_bf[:])
 
         def exp_decay(kind):
             for c in range(CLASSES):
@@ -115,14 +119,22 @@ def tile_tnlattention_pa_t_kernel(tc, q, k, v, log_slope, out):
                 )
 
         def mask_decay(kind, c):
-            nc.vector.scalar_tensor_tensor(
-                out=decay[:, kind, c, :],
-                in0=ramp[:],
-                scalar=nearer[:, c, kind : kind + 1],
-                in1=decay[:, kind, c, :],
-                op0=mybir.AluOpType.is_ge,
-                op1=mybir.AluOpType.mult,
-            )
+            if kind == 0:
+                parts = [(0, HALF_P, 0), (HALF_P, P, 0)]
+            elif kind == 1:
+                parts = [(0, P, HALF_SEQ)]
+            else:
+                parts = [(0, HALF_P, 0)]
+            for first, end, base in parts:
+                nc.gpsimd.affine_select(
+                    out=decay[first:end, kind, c, :],
+                    in_=decay[first:end, kind, c, :],
+                    pattern=[[CLASSES, P], [-1, PACK]],
+                    compare_op=mybir.AluOpType.is_ge,
+                    fill=0.0,
+                    base=base + c,
+                    channel_multiplier=-PACK,
+                )
 
         flipped = {}
         qk_t = {}
@@ -171,7 +183,7 @@ def tile_tnlattention_pa_t_kernel(tc, q, k, v, log_slope, out):
 
         def energy(b, spot):
             kind, c = ORDER[spot // CLASSES], spot % CLASSES
-            product = psum_e.tile([P, PACK, P], F32)
+            product = psum_e.tile([P, PACK, P], F32, name="product")
             for t in range(PACK):
                 if kind == 0:
                     for h in range(HEADS):
@@ -224,13 +236,12 @@ def tile_tnlattention_pa_t_kernel(tc, q, k, v, log_slope, out):
             out_sb[b] = store.tile([P, HEADS, HALVES, CLASSES, WIDTH], F32, name="out_sb")
             nc.scalar.copy(out=out_sb[b][:, :, 0, :, :], in_=shared[:].rearrange("m c h d -> m h c d"))
 
-        def output_own(b, heads, copy):
-            own = psum_o.tile([P, HEADS, CLASSES, WIDTH], F32, name="result")
-            for h in heads:
+        def output_own(b, heads, own, copy):
+            for n, h in enumerate(heads):
                 for c in range(CLASSES):
                     columns = tile_of(1 + h, c)
                     nc.tensor.matmul_mx(
-                        out=own[:, h, c, :],
+                        out=own[:, n * CLASSES + c, :],
                         lhsT=e_words[b][:, columns].bitcast(FP8X4),
                         lhsT_scale=e_scales[b][:, columns],
                         rhs=v_words[b][:, h, :].bitcast(FP8X4),
@@ -238,14 +249,18 @@ def tile_tnlattention_pa_t_kernel(tc, q, k, v, log_slope, out):
                         start=True,
                         stop=True,
                     )
-            some = slice(heads[0], heads[-1] + 1)
-            copy(out=out_sb[b][:, some, 1, :, :], in_=own[:, some, :, :])
+            copy(
+                out=out_sb[b][:, heads[0] : heads[-1] + 1, 1, :, :],
+                in_=own[:, 0 : len(heads) * CLASSES, :].rearrange("m (h c) d -> m h c d", c=CLASSES),
+            )
+
+        def output_rest(b):
+            own = psum_o.tile([P, HEADS * CLASSES, WIDTH], F32, name="result")
+            output_own(b, [0, 1], own, nc.scalar.copy)
+            nc.sync.dma_start(out=rows_of_out(b), in_=out_sb[b][:].rearrange("m h a c d -> m (h a) c d"))
 
         def rows_of_out(b):
             return out[b].rearrange("h n d -> (h n) d").rearrange("(g m c) d -> m g c d", m=P, c=CLASSES)
-
-        def store_out(b):
-            nc.sync.dma_start(out=rows_of_out(b), in_=out_sb[b][:].rearrange("m h a c d -> m (h a) c d"))
 
         exp_decay(1)
         transpose_q(0, 0)
@@ -261,6 +276,8 @@ def tile_tnlattention_pa_t_kernel(tc, q, k, v, log_slope, out):
                     mask_decay(ORDER[spot // CLASSES], spot % CLASSES)
                 energy(b, spot)
                 if spot == 0:
+                    if b + 1 < BUFS:
+                        zero(b + 1)
                     if b == 0:
                         transpose_q(0, 1)
                         transpose_k(0, 1)
@@ -270,31 +287,36 @@ def tile_tnlattention_pa_t_kernel(tc, q, k, v, log_slope, out):
                         quantise_energy(b - 1, 4, 6)
                     if b >= 2:
                         output_shared(b - 2)
-                if spot == 1 and b < last:
-                    transpose_q(b + 1, 0)
-                if spot == 2 and b < last:
-                    transpose_k(b + 1, 0)
+                if spot == 1:
+                    if b < last:
+                        transpose_q(b + 1, 0)
+                    else:
+                        output_rest(b - 2)
+                if spot == 2:
+                    if b < last:
+                        transpose_k(b + 1, 0)
+                    else:
+                        output_shared(b - 1)
                 if spot == 3:
                     quantise_v(b)
                     pad_v(b)
-                    if b >= 2:
-                        output_own(b - 2, [0, 1], nc.scalar.copy)
-                        store_out(b - 2)
+                    if 2 <= b < last:
+                        output_rest(b - 2)
                 if spot == 4:
                     quantise_energy(b, 0, 4)
                     if b < last:
                         regroup_v(b + 1)
                         transpose_q(b + 1, 1)
+                    else:
+                        output_rest(b - 1)
                 if spot == 5 and b < last:
                     transpose_k(b + 1, 1)
         quantise_energy(last, 4, 6)
-        output_shared(last - 1)
-        output_own(last - 1, [0, 1], nc.vector.tensor_copy)
-        store_out(last - 1)
         rows = rows_of_out(last)
         output_shared(last)
         for h in range(HEADS):
             nc.sync.dma_start(out=rows[:, h * HALVES, :, :], in_=out_sb[last][:, h, 0, :, :])
         for h in range(HEADS):
-            output_own(last, [h], nc.vector.tensor_copy if h == 0 else nc.scalar.copy)
+            own = psum_e.tile([P, PACK, P], F32, name="product")
+            output_own(last, [h], own, nc.scalar.copy if h == 0 else nc.vector.tensor_copy)
             nc.sync.dma_start(out=rows[:, h * HALVES + 1, :, :], in_=out_sb[last][:, h, 1, :, :])

@@ -23,6 +23,7 @@ HALF_SEQ = SEQ // HALVES
 KINDS = 1 + HEADS
 TILES = KINDS * CLASSES
 ORDER = [1, 0, 2]
+SPAN = PACK + CLASSES - 1
 PAIR = 2
 BUFS = 3
 
@@ -69,18 +70,17 @@ def tile_tnlattention_pa_t_kernel(tc, q, k, v, log_slope, out):
                     )
 
         identities = const.tile([P, 2, P], BF16)
-        ramp = const.tile([P, P * PACK], I32)
+        ramp = const.tile([P, P * SPAN], I32)
         make_identity(nc, identities[:, 0, :])
-        nc.gpsimd.iota(ramp[:], pattern=[[CLASSES, P], [-1, PACK]], base=0, channel_multiplier=-PACK)
+        nc.gpsimd.iota(ramp[:], pattern=[[CLASSES, P], [-1, SPAN]], base=1, channel_multiplier=-PACK)
         make_identity(nc, identities[:, 1, :])
         identity = identities[:, 0, :]
         exchange = identities[:].rearrange("p a n -> p (a n)")[:, HALF_P : HALF_P + P]
-        nearer = const.tile([P, CLASSES, KINDS], F32)
-        nc.vector.memset(nearer[:, 0, :], 0.0)
-        nc.vector.memset(nearer[HALF_P:P, 0, 0:1], -float(HALF_SEQ))
-        nc.vector.memset(nearer[:, 0, 1:2], -float(HALF_SEQ))
-        nc.vector.memset(nearer[HALF_P:P, 0, 2:3], -float(SEQ))
-        nc.vector.tensor_scalar_add(out=nearer[:, 1, :], in0=nearer[:, 0, :], scalar1=-1.0)
+        nearer = const.tile([P, KINDS], F32)
+        nc.vector.memset(nearer[:], 0.0)
+        nc.vector.memset(nearer[HALF_P:P, 0:1], -float(HALF_SEQ))
+        nc.vector.memset(nearer[:, 1:2], -float(HALF_SEQ))
+        nc.vector.memset(nearer[HALF_P:P, 2:3], -float(SEQ))
         k_half, v_half = [], []
         for i in range(BUFS):
             k_half.append(const.tile([P, HEADS, PACK, P], BF16, name="k_half%d" % i))
@@ -91,50 +91,39 @@ def tile_tnlattention_pa_t_kernel(tc, q, k, v, log_slope, out):
             nc.gpsimd.memset(v_half[i][:], 0)
 
         zero(0)
-        decay = const.tile([P, KINDS, CLASSES, P * PACK], F32)
+        decay = const.tile([P, KINDS, P * SPAN], F32)
         slope = const.tile([P, KINDS], F32)
         for kind in ORDER:
-            for c in range(CLASSES):
-                nc.vector.tensor_scalar(
-                    out=decay[:, kind, c, :],
-                    in0=ramp[:],
-                    scalar1=nearer[:, c, kind : kind + 1],
-                    scalar2=0.0,
-                    op0=mybir.AluOpType.subtract,
-                    op1=mybir.AluOpType.max,
-                )
+            nc.vector.tensor_scalar(
+                out=decay[:, kind, :],
+                in0=ramp[:],
+                scalar1=nearer[:, kind : kind + 1],
+                scalar2=0.0,
+                op0=mybir.AluOpType.subtract,
+                op1=mybir.AluOpType.max,
+            )
             if kind == ORDER[0]:
                 nc.vector.tensor_copy(out=slope[:, 1:KINDS], in_=slope_bf[:])
-            if kind == ORDER[1]:
                 nc.vector.tensor_copy(out=slope[0:HALF_P, 0:1], in_=slope_bf[0:HALF_P, 0:1])
                 nc.vector.tensor_copy(out=slope[HALF_P:P, 0:1], in_=slope_bf[HALF_P:P, 1:2])
 
         def exp_decay(kind):
-            for c in range(CLASSES):
-                nc.scalar.activation(
-                    out=decay[:, kind, c, :],
-                    in_=decay[:, kind, c, :],
-                    func=mybir.ActivationFunctionType.Exp,
-                    scale=slope[:, kind : kind + 1],
-                )
+            nc.scalar.activation(
+                out=decay[:, kind, :],
+                in_=decay[:, kind, :],
+                func=mybir.ActivationFunctionType.Exp,
+                scale=slope[:, kind : kind + 1],
+            )
 
-        def mask_decay(kind, c):
-            if kind == 0:
-                parts = [(0, HALF_P, 0), (HALF_P, P, 0)]
-            elif kind == 1:
-                parts = [(0, P, HALF_SEQ)]
-            else:
-                parts = [(0, HALF_P, 0)]
-            for first, end, base in parts:
-                nc.gpsimd.affine_select(
-                    out=decay[first:end, kind, c, :],
-                    in_=decay[first:end, kind, c, :],
-                    pattern=[[CLASSES, P], [-1, PACK]],
-                    compare_op=mybir.AluOpType.is_ge,
-                    fill=0.0,
-                    base=base + c,
-                    channel_multiplier=-PACK,
-                )
+        def mask_decay(kind):
+            nc.vector.scalar_tensor_tensor(
+                out=decay[:, kind, :],
+                in0=ramp[:],
+                scalar=nearer[:, kind : kind + 1],
+                in1=decay[:, kind, :],
+                op0=mybir.AluOpType.is_ge,
+                op1=mybir.AluOpType.mult,
+            )
 
         flipped = {}
         qk_t = {}
@@ -157,9 +146,14 @@ def tile_tnlattention_pa_t_kernel(tc, q, k, v, log_slope, out):
                     flipped[b, h][:, 1, t, :], k_sb[b][:, h, t, :], identity if h == 0 else exchange
                 )
             qk_t[b, h] = work.tile([P, 2, PACK, P], BF16, name="qk_t%d" % h)
-            nc.scalar.copy(out=qk_t[b, h][:], in_=flipped[b, h][:])
-            first_keys = slice(h * HALF_P, (h + 1) * HALF_P)
-            nc.scalar.copy(out=k_half[b % BUFS][:, h, :, first_keys], in_=flipped[b, h][:, 1, :, first_keys])
+            words = flipped[b, h][:].rearrange("d a n p -> d (a n p)").bitcast(F32)
+            nc.scalar.copy(out=qk_t[b, h][:].rearrange("d a n p -> d (a n p)").bitcast(F32), in_=words)
+            half = HALF_P // 2
+            k_words = words.rearrange("d (a n p) -> d a n p", a=2, n=PACK)[:, 1, :, h * half : (h + 1) * half]
+            target = k_half[b % BUFS][:, h, :, :].rearrange("d n p -> d (n p)").bitcast(F32)
+            nc.scalar.copy(
+                out=target.rearrange("d (n p) -> d n p", n=PACK)[:, :, h * half : (h + 1) * half], in_=k_words
+            )
 
         def regroup_v(b):
             v_grouped[b] = work.tile([P, HEADS, WIDTH, PACK], BF16, name="v_grouped", align_bytes=64)
@@ -205,7 +199,7 @@ def tile_tnlattention_pa_t_kernel(tc, q, k, v, log_slope, out):
             nc.vector.tensor_tensor(
                 out=grouped[b][:, spot, :, :],
                 in0=product[:].rearrange("p t m -> p m t"),
-                in1=decay[:, kind, c, :].rearrange("p (m t) -> p m t", t=PACK),
+                in1=decay[:, kind, :].rearrange("p (m u) -> p m u", u=SPAN)[:, :, 1 - c : 1 - c + PACK],
                 op=mybir.AluOpType.mult,
             )
 
@@ -272,8 +266,8 @@ def tile_tnlattention_pa_t_kernel(tc, q, k, v, log_slope, out):
             e_words[b] = work.tile([P, TILES * P], U32, name="e_words", align_bytes=64)
             e_scales[b] = work.tile([P, TILES * P], U8, name="e_scales", align_bytes=64)
             for spot in range(TILES):
-                if b == 0:
-                    mask_decay(ORDER[spot // CLASSES], spot % CLASSES)
+                if b == 0 and spot % CLASSES == 0:
+                    mask_decay(ORDER[spot // CLASSES])
                 energy(b, spot)
                 if spot == 0:
                     if b + 1 < BUFS:

from contextlib import ExitStack

import concourse.mybir as mybir
from concourse.masks import make_identity

BF16 = mybir.dt.bfloat16
F32 = mybir.dt.float32
I32 = mybir.dt.int32
U32 = mybir.dt.uint32
U8 = mybir.dt.uint8
FP8X4 = mybir.dt.float8_e4m3fn_x4

P = 128
HALF_P = P // 2
PACK = 4
BATCHES = 16
HEADS = 2
SEQ = 512
WIDTH = 128
HALVES = 2
CLASSES = 2
HALF_SEQ = SEQ // HALVES
KINDS = 1 + HEADS
TILES = KINDS * CLASSES
ORDER = [1, 0, 2]
SPAN = PACK + CLASSES - 1
PAIR = 2
BUFS = 3

FLOPS = 2 * 2 * BATCHES * HEADS * SEQ * SEQ * WIDTH


def tile_tnlattention_pa_t_kernel(tc, q, k, v, log_slope, out):
    nc = tc.nc
    with ExitStack() as ctx:
        const = ctx.enter_context(tc.tile_pool(name="const", bufs=1))
        resident = ctx.enter_context(tc.tile_pool(name="resident", bufs=1))
        work = ctx.enter_context(tc.tile_pool(name="work", bufs=BUFS))
        store = ctx.enter_context(tc.tile_pool(name="store", bufs=6))
        psum_t = ctx.enter_context(tc.psum_pool(name="psum_t", bufs=1))
        psum_e = ctx.enter_context(tc.psum_pool(name="psum_e", bufs=6))
        psum_o = ctx.enter_context(tc.psum_pool(name="psum_o", bufs=1))
        ctx.enter_context(tc.manual_schedule())

        slope_bf = const.tile([P, HEADS], BF16)
        nc.scalar.dma_start(out=slope_bf[:], in_=log_slope.partition_broadcast(P))
        q_sb, k_sb, v_sb = [], [], []
        for b in range(BATCHES):
            q_sb.append(resident.tile([P, HEADS * HALVES, CLASSES, WIDTH], BF16, name="q%d" % b))
            k_sb.append(resident.tile([P, HEADS, PACK, WIDTH], BF16, name="k%d" % b))
            for heads in [slice(0, 1), slice(1, 2)] if b == 0 else [slice(0, HEADS)]:
                nc.sync.dma_start(
                    out=q_sb[b][:, heads.start * HALVES : heads.stop * HALVES, :, :],
                    in_=q[b, heads].rearrange("h n d -> (h n) d").rearrange("(g m c) d -> m g c d", m=P, c=CLASSES),
                )
                nc.sync.dma_start(
                    out=k_sb[b][:, heads, :, :], in_=k[b, heads].rearrange("h (p t) d -> p h t d", t=PACK)
                )
            if b % PAIR == 0:
                v_sb.append(resident.tile([P, HEADS, PAIR, PACK, WIDTH], BF16, name="v%d" % b))
                pair = v[b : b + PAIR]
                target = v_sb[b // PAIR]
                nc.sync.dma_start(out=target[:, 0, :, :, :], in_=pair[:, 0].rearrange("b (p t) d -> p b t d", t=PACK))
                for x in range(2):
                    nc.sync.dma_start(
                        out=target[x * HALF_P : (x + 1) * HALF_P, 1, :, :, :],
                        in_=pair[:, 1, (1 - x) * HALF_SEQ : (2 - x) * HALF_SEQ].rearrange(
                            "b (p t) d -> p b t d", t=PACK
                        ),
                    )

        identities = const.tile([P, 2, P], BF16)
        ramp = const.tile([P, P * SPAN], I32)
        make_identity(nc, identities[:, 0, :])
        nc.gpsimd.iota(ramp[:], pattern=[[CLASSES, P], [-1, SPAN]], base=1, channel_multiplier=-PACK)
        make_identity(nc, identities[:, 1, :])
        identity = identities[:, 0, :]
        exchange = identities[:].rearrange("p a n -> p (a n)")[:, HALF_P : HALF_P + P]
        nearer = const.tile([P, KINDS], F32)
        nc.vector.memset(nearer[:], 0.0)
        nc.vector.memset(nearer[HALF_P:P, 0:1], -float(HALF_SEQ))
        nc.vector.memset(nearer[:, 1:2], -float(HALF_SEQ))
        nc.vector.memset(nearer[HALF_P:P, 2:3], -float(SEQ))
        k_half, v_half = [], []
        for i in range(BUFS):
            k_half.append(const.tile([P, HEADS, PACK, P], BF16, name="k_half%d" % i))
            v_half.append(const.tile([P, HEADS, WIDTH], U32, name="v_half%d" % i, align_bytes=64))

        def zero(i):
            nc.gpsimd.memset(k_half[i][:].rearrange("p h t n -> p (h t n)").bitcast(U32), 0)
            nc.gpsimd.memset(v_half[i][:], 0)

        zero(0)
        decay = const.tile([P, KINDS, P * SPAN], F32)
        slope = const.tile([P, KINDS], F32)
        for kind in ORDER:
            nc.vector.tensor_scalar(
                out=decay[:, kind, :],
                in0=ramp[:],
                scalar1=nearer[:, kind : kind + 1],
                scalar2=0.0,
                op0=mybir.AluOpType.subtract,
                op1=mybir.AluOpType.max,
            )
            if kind == ORDER[0]:
                nc.vector.tensor_copy(out=slope[:, 1:KINDS], in_=slope_bf[:])
                nc.vector.tensor_copy(out=slope[0:HALF_P, 0:1], in_=slope_bf[0:HALF_P, 0:1])
                nc.vector.tensor_copy(out=slope[HALF_P:P, 0:1], in_=slope_bf[HALF_P:P, 1:2])

        def exp_decay(kind):
            nc.scalar.activation(
                out=decay[:, kind, :],
                in_=decay[:, kind, :],
                func=mybir.ActivationFunctionType.Exp,
                scale=slope[:, kind : kind + 1],
            )

        def mask_decay(kind):
            nc.vector.scalar_tensor_tensor(
                out=decay[:, kind, :],
                in0=ramp[:],
                scalar=nearer[:, kind : kind + 1],
                in1=decay[:, kind, :],
                op0=mybir.AluOpType.is_ge,
                op1=mybir.AluOpType.mult,
            )

        flipped = {}
        qk_t = {}
        grouped = {}
        out_sb = {}
        e_words, e_scales = {}, {}
        v_grouped, v_words, v_scales = {}, {}, {}

        def transpose_q(b, h):
            flipped[b, h] = psum_t.tile([P, 2, PACK, P], BF16, name="flipped")
            for half in range(HALVES):
                for c in range(CLASSES):
                    nc.tensor.transpose(
                        flipped[b, h][:, 0, half * CLASSES + c, :], q_sb[b][:, h * HALVES + half, c, :], identity
                    )

        def transpose_k(b, h):
            for t in range(PACK):
                nc.tensor.transpose(
                    flipped[b, h][:, 1, t, :], k_sb[b][:, h, t, :], identity if h == 0 else exchange
                )
            qk_t[b, h] = work.tile([P, 2, PACK, P], BF16, name="qk_t%d" % h)
            words = flipped[b, h][:].rearrange("d a n p -> d (a n p)").bitcast(F32)
            nc.scalar.copy(out=qk_t[b, h][:].rearrange("d a n p -> d (a n p)").bitcast(F32), in_=words)
            half = HALF_P // 2
            k_words = words.rearrange("d (a n p) -> d a n p", a=2, n=PACK)[:, 1, :, h * half : (h + 1) * half]
            target = k_half[b % BUFS][:, h, :, :].rearrange("d n p -> d (n p)").bitcast(F32)
            nc.scalar.copy(
                out=target.rearrange("d (n p) -> d n p", n=PACK)[:, :, h * half : (h + 1) * half], in_=k_words
            )

        def regroup_v(b):
            v_grouped[b] = work.tile([P, HEADS, WIDTH, PACK], BF16, name="v_grouped", align_bytes=64)
            nc.scalar.copy(
                out=v_grouped[b][:], in_=v_sb[b // PAIR][:, :, b % PAIR, :, :].rearrange("p h t d -> p h d t")
            )

        def quantise_v(b):
            v_words[b] = work.tile([P, HEADS, WIDTH], U32, name="v_words", align_bytes=64)
            v_scales[b] = work.tile([P, HEADS, WIDTH], U8, name="v_scales", align_bytes=64)
            nc.vector.quantize_mx(
                out=v_words[b][:].rearrange("p h d -> p (h d)").bitcast(FP8X4),
                scales=v_scales[b][:].rearrange("p h d -> p (h d)"),
                in_=v_grouped[b][:].rearrange("p h d t -> p (h d t)"),
            )

        def pad_v(b):
            for h in range(HEADS):
                rows = slice(h * HALF_P, (h + 1) * HALF_P)
                nc.gpsimd.tensor_copy(out=v_half[b % BUFS][rows, h, :], in_=v_words[b][rows, h, :])

        def energy(b, spot):
            kind, c = ORDER[spot // CLASSES], spot % CLASSES
            product = psum_e.tile([P, PACK, P], F32, name="product")
            for t in range(PACK):
                if kind == 0:
                    for h in range(HEADS):
                        nc.tensor.matmul(
                            out=product[:, t, :],
                            lhsT=k_half[b % BUFS][:, h, t, :],
                            rhs=qk_t[b, h][:, 0, c, :],
                            start=(h == 0),
                            stop=(h == HEADS - 1),
                        )
                else:
                    nc.tensor.matmul(
                        out=product[:, t, :],
                        lhsT=qk_t[b, kind - 1][:, 1, t, :],
                        rhs=qk_t[b, kind - 1][:, 0, CLASSES + c, :],
                        start=True,
                        stop=True,
                    )
            nc.vector.tensor_tensor(
                out=grouped[b][:, spot, :, :],
                in0=product[:].rearrange("p t m -> p m t"),
                in1=decay[:, kind, :].rearrange("p (m u) -> p m u", u=SPAN)[:, :, 1 - c : 1 - c + PACK],
                op=mybir.AluOpType.mult,
            )

        def quantise_energy(b, first, last):
            nc.vector.quantize_mx(
                out=e_words[b][:, first * P : last * P].bitcast(FP8X4),
                scales=e_scales[b][:, first * P : last * P],
                in_=grouped[b][:, first:last, :, :].rearrange("p n m t -> p (n m t)"),
            )

        def tile_of(kind, c):
            first = (ORDER.index(kind) * CLASSES + c) * P
            return slice(first, first + P)

        def output_shared(b):
            shared = psum_o.tile([P, CLASSES, HEADS, WIDTH], F32, name="result")
            for c in range(CLASSES):
                columns = tile_of(0, c)
                nc.tensor.matmul_mx(
                    out=shared[:, c, :, :].rearrange("m h d -> m (h d)"),
                    lhsT=e_words[b][:, columns].bitcast(FP8X4),
                    lhsT_scale=e_scales[b][:, columns],
                    rhs=v_half[b % BUFS][:].rearrange("p h d -> p (h d)").bitcast(FP8X4),
                    rhs_scale=v_scales[b][:].rearrange("p h d -> p (h d)"),
                    start=True,
                    stop=True,
                )
            out_sb[b] = store.tile([P, HEADS, HALVES, CLASSES, WIDTH], F32, name="out_sb")
            nc.scalar.copy(out=out_sb[b][:, :, 0, :, :], in_=shared[:].rearrange("m c h d -> m h c d"))

        def output_own(b, heads, own, copy):
            for n, h in enumerate(heads):
                for c in range(CLASSES):
                    columns = tile_of(1 + h, c)
                    nc.tensor.matmul_mx(
                        out=own[:, n * CLASSES + c, :],
                        lhsT=e_words[b][:, columns].bitcast(FP8X4),
                        lhsT_scale=e_scales[b][:, columns],
                        rhs=v_words[b][:, h, :].bitcast(FP8X4),
                        rhs_scale=v_scales[b][:, h, :],
                        start=True,
                        stop=True,
                    )
            copy(
                out=out_sb[b][:, heads[0] : heads[-1] + 1, 1, :, :],
                in_=own[:, 0 : len(heads) * CLASSES, :].rearrange("m (h c) d -> m h c d", c=CLASSES),
            )

        def output_rest(b):
            own = psum_o.tile([P, HEADS * CLASSES, WIDTH], F32, name="result")
            output_own(b, [0, 1], own, nc.scalar.copy)
            nc.sync.dma_start(out=rows_of_out(b), in_=out_sb[b][:].rearrange("m h a c d -> m (h a) c d"))

        def rows_of_out(b):
            return out[b].rearrange("h n d -> (h n) d").rearrange("(g m c) d -> m g c d", m=P, c=CLASSES)

        exp_decay(1)
        transpose_q(0, 0)
        transpose_k(0, 0)
        exp_decay(0)
        last = BATCHES - 1
        for b in range(BATCHES):
            grouped[b] = work.tile([P, TILES, P, PACK], BF16, name="grouped", align_bytes=64)
            e_words[b] = work.tile([P, TILES * P], U32, name="e_words", align_bytes=64)
            e_scales[b] = work.tile([P, TILES * P], U8, name="e_scales", align_bytes=64)
            for spot in range(TILES):
                if b == 0 and spot % CLASSES == 0:
                    mask_decay(ORDER[spot // CLASSES])
                energy(b, spot)
                if spot == 0:
                    if b + 1 < BUFS:
                        zero(b + 1)
                    if b == 0:
                        transpose_q(0, 1)
                        transpose_k(0, 1)
                        regroup_v(0)
                        exp_decay(2)
                    if b >= 1:
                        quantise_energy(b - 1, 4, 6)
                    if b >= 2:
                        output_shared(b - 2)
                if spot == 1:
                    if b < last:
                        transpose_q(b + 1, 0)
                    else:
                        output_rest(b - 2)
                if spot == 2:
                    if b < last:
                        transpose_k(b + 1, 0)
                    else:
                        output_shared(b - 1)
                if spot == 3:
                    quantise_v(b)
                    pad_v(b)
                    if 2 <= b < last:
                        output_rest(b - 2)
                if spot == 4:
                    quantise_energy(b, 0, 4)
                    if b < last:
                        regroup_v(b + 1)
                        transpose_q(b + 1, 1)
                    else:
                        output_rest(b - 1)
                if spot == 5 and b < last:
                    transpose_k(b + 1, 1)
        quantise_energy(last, 4, 6)
        rows = rows_of_out(last)
        output_shared(last)
        for h in range(HEADS):
            nc.sync.dma_start(out=rows[:, h * HALVES, :, :], in_=out_sb[last][:, h, 0, :, :])
        for h in range(HEADS):
            own = psum_e.tile([P, PACK, P], F32, name="product")
            output_own(last, [h], own, nc.scalar.copy if h == 0 else nc.vector.tensor_copy)
            nc.sync.dma_start(out=rows[:, h * HALVES + 1, :, :], in_=out_sb[last][:, h, 1, :, :])
